import numpy as np
import ml_dtypes


def mxq(x, axis, fmt="e4m3"):
    dtype, down = {"e4m3": (ml_dtypes.float8_e4m3fn, 7), "e5m2": (ml_dtypes.float8_e5m2, 14)}[fmt]
    v = np.moveaxis(np.asarray(x, np.float32).astype(ml_dtypes.bfloat16).astype(np.float64), axis, -1)
    blocks = v.reshape(v.shape[:-1] + (-1, 32))
    amax = np.abs(blocks).max(-1, keepdims=True)
    byte = np.maximum(np.where(amax > 0, np.frexp(amax)[1] - 1 + 127, 0) - down, 1)
    scale = np.exp2(byte - 127.0)
    codes = (blocks / scale).astype(np.float32).astype(dtype).astype(np.float64)
    return np.moveaxis((codes * scale).reshape(v.shape), -1, axis)


WIDE = False


def mx_kscale(k):
    if not WIDE:
        return np.ones(k)
    levels = np.array([10, -10, 5, -5, 0])
    a = np.random.permutation(np.resize(levels, k // 512 * 4)).reshape(k // 512, 4)
    idx = np.arange(k)
    return np.exp2(a[idx // 512, idx % 128 // 32])


BF16 = ml_dtypes.bfloat16


def bf(x):
    return np.asarray(x, np.float32).astype(BF16)


def f64(x):
    return np.asarray(x).astype(np.float64)


B, E, D = 256, 2048, 2048


def setup_inputs():
    s = mx_kscale(E)
    ws = 1.0 / np.sqrt(E)
    return {
        "x": bf(np.random.standard_normal((B, E)) * s),
        "state_A": bf(np.random.uniform(0.0, 1.0, (B, D))),
        "state_B": bf(0.5 + np.random.uniform(0.0, 1.0, (B, D))),
        "state_p": bf(np.random.standard_normal((B, D))),
        "state_x": bf(np.random.standard_normal((B, E)) * s),
        "time_decay": bf(0.5 * np.random.standard_normal(D)),
        "time_first": bf(np.log(0.3) + 0.3 * np.random.standard_normal(D)),
        "time_mix_k": bf(np.random.uniform(0.0, 1.0, (1, E))),
        "time_mix_v": bf(np.random.uniform(0.0, 1.0, (1, E))),
        "W_key": bf(np.random.standard_normal((D, E)) * ws / s[None, :]),
        "W_value": bf(np.random.standard_normal((D, E)) * ws / s[None, :]),
    }


def reference(x, state_A, state_B, state_p, state_x, time_decay, time_first, time_mix_k, time_mix_v, W_key, W_value):
    x, state_x = f64(x), f64(state_x)
    state_A, state_B, state_p = f64(state_A), f64(state_B), f64(state_p)
    mk, mv = f64(time_mix_k), f64(time_mix_v)
    xk = x * mk + state_x * (1.0 - mk)
    xv = x * mv + state_x * (1.0 - mv)
    k = mxq(xk, 1, "e4m3") @ mxq(f64(W_key), 1, "e4m3").T
    v = mxq(xv, 1, "e4m3") @ mxq(f64(W_value), 1, "e4m3").T
    ww = f64(time_first) + k
    p = np.maximum(state_p, ww)
    e1 = np.exp(state_p - p)
    e2 = np.exp(ww - p)
    a = e1 * state_A + e2 * v
    b = e1 * state_B + e2
    td = -np.exp(f64(time_decay))
    ww = state_p + td
    p = np.maximum(ww, k)
    e1 = np.exp(ww - p)
    e2 = np.exp(k - p)
    new_A = e1 * state_A + e2 * v
    new_B = e1 * state_B + e2
    return (a, b, new_A, new_B, p)

@@ -1,0 +1,287 @@
+from contextlib import ExitStack
+
+import concourse.mybir as mybir
+from concourse.masks import make_identity
+
+F32 = mybir.dt.float32
+BF16 = mybir.dt.bfloat16
+U32 = mybir.dt.uint32
+U8 = mybir.dt.uint8
+FP8X4 = mybir.dt.float8_e4m3fn_x4
+ALU = mybir.AluOpType
+ACT = mybir.ActivationFunctionType
+
+P = 128
+ROWS = 256
+E = 2048
+D = 2048
+NT = 512
+FLOPS = 2 * 2 * ROWS * E * D
+
+
+def tile_rwkv_timemix_for_quant_pa_kernel(
+    tc,
+    x,
+    state_A,
+    state_B,
+    state_p,
+    state_x,
+    time_decay,
+    time_first,
+    time_mix_k,
+    time_mix_v,
+    W_key,
+    W_value,
+    out_0,
+    out_1,
+    out_2,
+    out_3,
+    out_4,
+):
+    nc = tc.nc
+    with ExitStack() as ctx:
+        const = ctx.enter_context(tc.tile_pool(name="const", bufs=1))
+        ring = ctx.enter_context(tc.tile_pool(name="ring", bufs=8))
+        grp = ctx.enter_context(tc.tile_pool(name="grp", bufs=3))
+        cod = ctx.enter_context(tc.tile_pool(name="cod", bufs=3))
+        st = ctx.enter_context(tc.tile_pool(name="st", bufs=2))
+        ep = ctx.enter_context(tc.tile_pool(name="ep", bufs=2))
+        tp = ctx.enter_context(tc.psum_pool(name="tp", bufs=4))
+        acc = ctx.enter_context(tc.psum_pool(name="acc", bufs=4))
+
+        weights = (W_key, W_value)
+
+        mkb = const.tile([P, 32], BF16, name="mkb")
+        with nc.allow_non_contiguous_dma(reason="mix coefficients, two neighbouring k to a partition"):
+            nc.scalar.dma_start(
+                out=mkb[:, 0:16].rearrange("p (a e) -> p a e", e=2),
+                in_=time_mix_k.rearrange("o (a p e) -> p (o a) e", a=8, p=P, e=2),
+            )
+            nc.gpsimd.dma_start(
+                out=mkb[:, 16:32].rearrange("p (a e) -> p a e", e=2),
+                in_=time_mix_v.rearrange("o (a p e) -> p (o a) e", a=8, p=P, e=2),
+            )
+
+        x_sb = ring.tile([P, 4096], BF16, tag="ring", name="x_sb")
+        nc.sync.dma_start(
+            out=x_sb[:].rearrange("p (r k) -> p r k", r=2),
+            in_=x.rearrange("(r p) k -> p r k", p=P),
+        )
+        sx_sb = ring.tile([P, 4096], BF16, tag="ring", name="sx_sb")
+        nc.sync.dma_start(
+            out=sx_sb[:].rearrange("p (r k) -> p r k", r=2),
+            in_=state_x.rearrange("(r p) k -> p r k", p=P),
+        )
+
+        ident = const.tile([P, P], F32, name="ident")
+        make_identity(nc, ident[:])
+
+        def load_w(v, j):
+            halves = []
+            for h in range(2):
+                wr = ring.tile([P, 4096], BF16, tag="ring", name="wr")
+                row0 = NT * j + 256 * h
+                nc.sync.dma_start(
+                    out=wr[:].rearrange("p (c k) -> p c k", c=2),
+                    in_=weights[v][row0 : row0 + 256, :].rearrange("(c p) k -> p c k", p=P),
+                )
+                halves.append(wr)
+            return halves
+
+        def load_states(j):
+            tiles = []
+            for src in (state_p, state_A, state_B):
+                t = st.tile([P, 1024], BF16, tag="st%d" % len(tiles), name="st_t")
+                nc.sync.dma_start(
+                    out=t[:].rearrange("p (r d) -> p r d", r=2),
+                    in_=src.rearrange("(r p) d -> p r d", p=P)[:, :, NT * j : NT * (j + 1)],
+                )
+                tiles.append(t)
+            return tiles
+
+        raw_w = {}
+        raw_w[(0, 0)] = load_w(0, 0)
+        raw_w[(1, 0)] = load_w(1, 0)
+
+        tftd = ring.tile([P, 4096], BF16, tag="ring", name="tftd")
+        nc.sync.dma_start(out=tftd[:, 0:2048], in_=time_first.partition_broadcast(P))
+        nc.sync.dma_start(out=tftd[:, 2048:4096], in_=time_decay.partition_broadcast(P))
+        states = {}
+        states[0] = load_states(0)
+
+        mkf = const.tile([P, 32], F32, name="mkf")
+        nc.vector.tensor_copy(out=mkf[:], in_=mkb[:])
+
+        sxg = ring.tile([P, 4096], BF16, tag="ring", name="sxg")
+        sxg_w = sxg[:].bitcast(F32)
+        xg = grp.tile([P, 8192], BF16, tag="grp", name="xg", align_bytes=64)
+        xw = x_sb[:].bitcast(F32)
+        sw = sx_sb[:].bitcast(F32)
+        for g in range(4):
+            xb = tp.tile([P, 512], F32, tag="tp", name="xb")
+            sb = tp.tile([P, 512], F32, tag="tp", name="sb")
+            for u in range(2):
+                for r in range(2):
+                    col = 256 * u + 128 * r
+                    src = 1024 * r + 256 * g + 128 * u
+                    nc.tensor.transpose(sb[:, col : col + 128], sw[:, src : src + 128], ident[:])
+                    nc.tensor.transpose(xb[:, col : col + 128], xw[:, src : src + 128], ident[:])
+            nc.scalar.copy(
+                out=sxg_w[:, 512 * g : 512 * (g + 1)].rearrange("p (n u) -> p n u", u=2),
+                in_=sb[:].rearrange("p (u n) -> p n u", u=2),
+            )
+            sx_g = sxg[:, 1024 * g : 1024 * (g + 1)]
+            dx = ep.tile([P, 1024], F32, tag="ndd", name="dx")
+            nc.vector.tensor_tensor(
+                out=dx[:].rearrange("p (n u e) -> p n u e", u=2, e=2),
+                in0=xb[:].bitcast(BF16).rearrange("p (u n e) -> p n u e", u=2, e=2),
+                in1=sx_g.rearrange("p (n u e) -> p n u e", u=2, e=2),
+                op=ALU.subtract,
+            )
+            for v in range(2):
+                y = ep.tile([P, 1024], F32, tag="xf%d" % v, name="y")
+                nc.vector.tensor_tensor(
+                    out=y[:].rearrange("p (n t) -> p n t", t=4),
+                    in0=dx[:].rearrange("p (n t) -> p n t", t=4),
+                    in1=mkf[:, 16 * v + 4 * g : 16 * v + 4 * g + 4].unsqueeze(1).to_broadcast([P, 256, 4]),
+                    op=ALU.mult,
+                )
+                o0 = 4096 * v + 1024 * g
+                nc.vector.tensor_tensor(out=xg[:, o0 : o0 + 1024], in0=y[:], in1=sx_g, op=ALU.add)
+
+        xcodes = const.tile([P, 2048], U32, name="xcodes", align_bytes=64)
+        xscl = const.tile([P, 2048], U8, name="xscl", align_bytes=64)
+        for v in range(2):
+            nc.vector.quantize_mx(
+                out=xcodes[:, 1024 * v : 1024 * (v + 1)].bitcast(FP8X4),
+                scales=xscl[:, 1024 * v : 1024 * (v + 1)],
+                in_=xg[:, 4096 * v : 4096 * (v + 1)],
+            )
+
+        tfw = const.tile([P, 4096], F32, name="tfw")
+        nc.scalar.copy(out=tfw[:, 0:2048], in_=tftd[:, 0:2048])
+        nc.scalar.activation(out=tfw[:, 2048:4096], in_=tftd[:, 2048:4096], func=ACT.Exp)
+        tfw_v = tfw[:].rearrange("p (h d) -> p h d", h=2)
+
+        def prep_w(v, j):
+            halves = raw_w[(v, j)]
+            gt = grp.tile([P, 8192], BF16, tag="grp", name="gt", align_bytes=64)
+            gw = gt[:].bitcast(F32).rearrange("p (g d u) -> p g d u", g=4, d=NT, u=2)
+            codes = cod.tile([P, 2048], U32, tag="codes", name="codes", align_bytes=64)
+            scl = cod.tile([P, 2048], U8, tag="scl", name="scl", align_bytes=64)
+            for c in range(4):
+                wf = halves[c // 2][:].bitcast(F32)
+                base = 1024 * (c % 2)
+                for hb in range(2):
+                    bank = tp.tile([P, 512], F32, tag="tp", name="bank")
+                    for gi in range(2):
+                        for u in range(2):
+                            src = base + 256 * (2 * hb + gi) + 128 * u
+                            col = 128 * (2 * gi + u)
+                            nc.tensor.transpose(bank[:, col : col + 128], wf[:, src : src + 128], ident[:])
+                    nc.scalar.copy(
+                        out=gw[:, 2 * hb : 2 * hb + 2, 128 * c : 128 * (c + 1), :],
+                        in_=bank[:].rearrange("p (g u d) -> p g d u", g=2, u=2, d=128),
+                    )
+            for hb in range(2):
+                nc.vector.quantize_mx(
+                    out=codes[:, 1024 * hb : 1024 * (hb + 1)].bitcast(FP8X4),
+                    scales=scl[:, 1024 * hb : 1024 * (hb + 1)],
+                    in_=gt[:, 4096 * hb : 4096 * (hb + 1)],
+                )
+            return codes, scl
+
+        def project(wq, r):
+            banks = []
+            for v in range(2):
+                codes, scl = wq[v]
+                ps = acc.tile([P, NT], F32, tag="acc", name="ps")
+                for g in range(4):
+                    c0 = 1024 * v + 256 * g + 128 * r
+                    nc.tensor.matmul_mx(
+                        out=ps[:],
+                        lhsT=xcodes[:, c0 : c0 + 128].bitcast(FP8X4),
+                        lhsT_scale=xscl[:, c0 : c0 + 128],
+                        rhs=codes[:, NT * g : NT * (g + 1)].bitcast(FP8X4),
+                        rhs_scale=scl[:, NT * g : NT * (g + 1)],
+                        start=(g == 0),
+                        stop=(g == 3),
+                    )
+                banks.append(ps)
+            return banks
+
+        def front(j, r, k_ps):
+            sp_t = states[j][0]
+            nq = ep.tile([P, NT], F32, tag="nq", name="nq")
+            nc.vector.tensor_tensor(out=nq[:], in0=sp_t[:, NT * r : NT * (r + 1)], in1=k_ps[:], op=ALU.subtract)
+            ndd = ep.tile([P, 1024], F32, tag="ndd", name="ndd")
+            nc.vector.tensor_tensor(
+                out=ndd[:].rearrange("p (h d) -> p h d", h=2),
+                in0=nq[:].unsqueeze(1).to_broadcast([P, 2, NT]),
+                in1=tfw_v[:, :, NT * j : NT * (j + 1)],
+                op=ALU.subtract,
+            )
+            p2 = ep.tile([P, NT], F32, tag="p2", name="p2")
+            nc.vector.scalar_tensor_tensor(
+                out=p2[:], in0=ndd[:, NT : 2 * NT], scalar=0.0, in1=k_ps[:], op0=ALU.max, op1=ALU.add
+            )
+            nc.gpsimd.dma_start(out=out_4[P * r : P * (r + 1), NT * j : NT * (j + 1)], in_=p2[:])
+            xf1 = ep.tile([P, 1024], F32, tag="xf0", name="xf1")
+            nc.scalar.activation(out=xf1[:], in_=ndd[:], func=ACT.Exp)
+            xf2 = ep.tile([P, 1024], F32, tag="xf1", name="xf2")
+            nc.scalar.activation(out=xf2[:], in_=ndd[:], func=ACT.Exp, scale=-1.0)
+            return xf1, xf2
+
+        def back(j, r, v_ps, xf1, xf2):
+            a_t = states[j][1]
+            b_t = states[j][2]
+            two = "p (h d) -> p h d"
+            t1 = ep.tile([P, 1024], F32, tag="t1", name="t1")
+            nc.vector.scalar_tensor_tensor(
+                out=t1[:].rearrange(two, h=2),
+                in0=xf1[:].rearrange(two, h=2),
+                scalar=1.0,
+                in1=a_t[:, NT * r : NT * (r + 1)].unsqueeze(1).to_broadcast([P, 2, NT]),
+                op0=ALU.min,
+                op1=ALU.mult,
+            )
+            t2 = ep.tile([P, 1024], F32, tag="t2", name="t2")
+            nc.vector.scalar_tensor_tensor(
+                out=t2[:].rearrange(two, h=2),
+                in0=xf2[:].rearrange(two, h=2),
+                scalar=1.0,
+                in1=v_ps[:].unsqueeze(1).to_broadcast([P, 2, NT]),
+                op0=ALU.min,
+                op1=ALU.mult,
+            )
+            nc.vector.tensor_tensor(out=t1[:], in0=t1[:], in1=t2[:], op=ALU.add)
+            rows = slice(P * r, P * (r + 1))
+            cols = slice(NT * j, NT * (j + 1))
+            nc.gpsimd.dma_start(out=out_0[rows, cols], in_=t1[:, 0:NT])
+            nc.gpsimd.dma_start(out=out_2[rows, cols], in_=t1[:, NT : 2 * NT])
+            nc.vector.scalar_tensor_tensor(
+                out=xf1[:].rearrange(two, h=2),
+                in0=xf1[:].rearrange(two, h=2),
+                scalar=1.0,
+                in1=b_t[:, NT * r : NT * (r + 1)].unsqueeze(1).to_broadcast([P, 2, NT]),
+                op0=ALU.min,
+                op1=ALU.mult,
+            )
+            nc.vector.scalar_tensor_tensor(
+                out=xf2[:], in0=xf2[:], scalar=1.0, in1=xf1[:], op0=ALU.min, op1=ALU.add
+            )
+            nc.gpsimd.dma_start(out=out_1[rows, cols], in_=xf2[:, 0:NT])
+            nc.gpsimd.dma_start(out=out_3[rows, cols], in_=xf2[:, NT : 2 * NT])
+
+        wq = (prep_w(0, 0), prep_w(1, 0))
+        for j in range(4):
+            if j + 1 < 4:
+                raw_w[(0, j + 1)] = load_w(0, j + 1)
+                raw_w[(1, j + 1)] = load_w(1, j + 1)
+                states[j + 1] = load_states(j + 1)
+            banks = [project(wq, r) for r in range(2)]
+            exps = [front(j, r, banks[r][0]) for r in range(2)]
+            if j + 1 < 4:
+                wq = (prep_w(0, j + 1), prep_w(1, j + 1))
+            for r in range(2):
+                back(j, r, banks[r][1], exps[r][0], exps[r][1])

@@ -16,6 +16,7 @@ ROWS = 256
 E = 2048
 D = 2048
 NT = 512
+TILES = D // NT
 FLOPS = 2 * 2 * ROWS * E * D
 
 
@@ -48,45 +49,20 @@ def tile_rwkv_timemix_for_quant_pa_kernel(
         ep = ctx.enter_context(tc.tile_pool(name="ep", bufs=2))
         tp = ctx.enter_context(tc.psum_pool(name="tp", bufs=4))
         acc = ctx.enter_context(tc.psum_pool(name="acc", bufs=4))
+        ctx.enter_context(tc.manual_schedule())
 
         weights = (W_key, W_value)
+        raw_w = {}
+        states = {}
 
-        mkb = const.tile([P, 32], BF16, name="mkb")
-        with nc.allow_non_contiguous_dma(reason="mix coefficients, two neighbouring k to a partition"):
-            nc.scalar.dma_start(
-                out=mkb[:, 0:16].rearrange("p (a e) -> p a e", e=2),
-                in_=time_mix_k.rearrange("o (a p e) -> p (o a) e", a=8, p=P, e=2),
+        def load_w(v, j, h):
+            wr = ring.tile([P, 4096], BF16, tag="ring", name="wr")
+            row0 = NT * j + 256 * h
+            nc.sync.dma_start(
+                out=wr[:].rearrange("p (c k) -> p c k", c=2),
+                in_=weights[v][row0 : row0 + 256, :].rearrange("(c p) k -> p c k", p=P),
             )
-            nc.gpsimd.dma_start(
-                out=mkb[:, 16:32].rearrange("p (a e) -> p a e", e=2),
-                in_=time_mix_v.rearrange("o (a p e) -> p (o a) e", a=8, p=P, e=2),
-            )
-
-        x_sb = ring.tile([P, 4096], BF16, tag="ring", name="x_sb")
-        nc.sync.dma_start(
-            out=x_sb[:].rearrange("p (r k) -> p r k", r=2),
-            in_=x.rearrange("(r p) k -> p r k", p=P),
-        )
-        sx_sb = ring.tile([P, 4096], BF16, tag="ring", name="sx_sb")
-        nc.sync.dma_start(
-            out=sx_sb[:].rearrange("p (r k) -> p r k", r=2),
-            in_=state_x.rearrange("(r p) k -> p r k", p=P),
-        )
-
-        ident = const.tile([P, P], F32, name="ident")
-        make_identity(nc, ident[:])
-
-        def load_w(v, j):
-            halves = []
-            for h in range(2):
-                wr = ring.tile([P, 4096], BF16, tag="ring", name="wr")
-                row0 = NT * j + 256 * h
-                nc.sync.dma_start(
-                    out=wr[:].rearrange("p (c k) -> p c k", c=2),
-                    in_=weights[v][row0 : row0 + 256, :].rearrange("(c p) k -> p c k", p=P),
-                )
-                halves.append(wr)
-            return halves
+            raw_w[(v, j, h)] = wr
 
         def load_states(j):
             tiles = []
@@ -97,80 +73,111 @@ def tile_rwkv_timemix_for_quant_pa_kernel(
                     in_=src.rearrange("(r p) d -> p r d", p=P)[:, :, NT * j : NT * (j + 1)],
                 )
                 tiles.append(t)
-            return tiles
+            states[j] = tiles
 
-        raw_w = {}
-        raw_w[(0, 0)] = load_w(0, 0)
-        raw_w[(1, 0)] = load_w(1, 0)
-
+        mkb = const.tile([P, 32], BF16, name="mkb")
+        with nc.allow_non_contiguous_dma(reason="mix coefficients, two neighbouring k to a partition"):
+            nc.sync.dma_start(
+                out=mkb[:, 0:16].rearrange("p (a e) -> p a e", e=2),
+                in_=time_mix_k.rearrange("o (a p e) -> p (o a) e", a=8, p=P, e=2),
+            )
+            nc.sync.dma_start(
+                out=mkb[:, 16:32].rearrange("p (a e) -> p a e", e=2),
+                in_=time_mix_v.rearrange("o (a p e) -> p (o a) e", a=8, p=P, e=2),
+            )
+        x_sb = ring.tile([P, 4096], BF16, tag="ring", name="x_sb")
+        sx_sb = ring.tile([P, 4096], BF16, tag="ring", name="sx_sb")
+        for g in range(4):
+            for dst, src in ((sx_sb, state_x), (x_sb, x)):
+                nc.sync.dma_start(
+                    out=dst[:, 1024 * g : 1024 * (g + 1)].rearrange("p (r k) -> p r k", r=2),
+                    in_=src.rearrange("(r p) k -> p r k", p=P)[:, :, 512 * g : 512 * (g + 1)],
+                )
+        for v in range(2):
+            for h in range(2):
+                load_w(v, 0, h)
         tftd = ring.tile([P, 4096], BF16, tag="ring", name="tftd")
         nc.sync.dma_start(out=tftd[:, 0:2048], in_=time_first.partition_broadcast(P))
         nc.sync.dma_start(out=tftd[:, 2048:4096], in_=time_decay.partition_broadcast(P))
-        states = {}
-        states[0] = load_states(0)
+        load_states(0)
+        load_w(0, 1, 0)
 
+        ident = const.tile([P, P], F32, name="ident")
+        make_identity(nc, ident[:])
+        identb = const.tile([P, P], BF16, name="identb")
+        make_identity(nc, identb[:])
+        nidentb = const.tile([P, P], BF16, name="nidentb")
+        nc.vector.tensor_scalar_mul(out=nidentb[:], in0=identb[:], scalar1=-1.0)
+        warm_in = const.tile([P, 1], F32, name="warm_in")
+        warm_out = const.tile([P, 1], F32, name="warm_out")
+        nc.vector.memset(warm_in[:], 0.0)
+        nc.scalar.activation(out=warm_out[:], in_=warm_in[:], func=ACT.Exp)
         mkf = const.tile([P, 32], F32, name="mkf")
         nc.vector.tensor_copy(out=mkf[:], in_=mkb[:])
 
-        sxg = ring.tile([P, 4096], BF16, tag="ring", name="sxg")
-        sxg_w = sxg[:].bitcast(F32)
         xg = grp.tile([P, 8192], BF16, tag="grp", name="xg", align_bytes=64)
-        xw = x_sb[:].bitcast(F32)
         sw = sx_sb[:].bitcast(F32)
         for g in range(4):
-            xb = tp.tile([P, 512], F32, tag="tp", name="xb")
             sb = tp.tile([P, 512], F32, tag="tp", name="sb")
             for u in range(2):
                 for r in range(2):
+                    src = 512 * g + 256 * r + 128 * u
                     col = 256 * u + 128 * r
-                    src = 1024 * r + 256 * g + 128 * u
                     nc.tensor.transpose(sb[:, col : col + 128], sw[:, src : src + 128], ident[:])
-                    nc.tensor.transpose(xb[:, col : col + 128], xw[:, src : src + 128], ident[:])
-            nc.scalar.copy(
-                out=sxg_w[:, 512 * g : 512 * (g + 1)].rearrange("p (n u) -> p n u", u=2),
-                in_=sb[:].rearrange("p (u n) -> p n u", u=2),
-            )
-            sx_g = sxg[:, 1024 * g : 1024 * (g + 1)]
-            dx = ep.tile([P, 1024], F32, tag="ndd", name="dx")
-            nc.vector.tensor_tensor(
-                out=dx[:].rearrange("p (n u e) -> p n u e", u=2, e=2),
-                in0=xb[:].bitcast(BF16).rearrange("p (u n e) -> p n u e", u=2, e=2),
-                in1=sx_g.rearrange("p (n u e) -> p n u e", u=2, e=2),
-                op=ALU.subtract,
-            )
+            sxs = ep.tile([P, 1024], BF16, tag="ndd", name="sxs")
+            nc.scalar.copy(out=sxs[:].bitcast(F32), in_=sb[:])
+            plns = [ep.tile([P, 1024], BF16, tag="t%d" % (v + 1), name="pln") for v in range(2)]
+            for u in range(2):
+                dxb = tp.tile([P, 512], F32, tag="tp", name="dxb")
+                for e in range(2):
+                    for r in range(2):
+                        base = 1024 * g + 512 * r + 256 * u
+                        col = 256 * e + 128 * r
+                        xs = x_sb[:, base : base + 256].rearrange("p (w e) -> p w e", e=2)[:, :, e]
+                        ss = sx_sb[:, base : base + 256].rearrange("p (w e) -> p w e", e=2)[:, :, e]
+                        nc.tensor.matmul(out=dxb[:, col : col + 128], lhsT=xs, rhs=identb[:], start=True, stop=False)
+                        nc.tensor.matmul(out=dxb[:, col : col + 128], lhsT=ss, rhs=nidentb[:], start=False, stop=True)
+                for e in range(2):
+                    t = 2 * u + e
+                    sx_pl = sxs[:, 512 * u : 512 * (u + 1)].rearrange("p (n e) -> p n e", e=2)[:, :, e]
+                    for v in range(2):
+                        i = 16 * v + 4 * g + t
+                        nc.vector.scalar_tensor_tensor(
+                            out=plns[v][:, 256 * t : 256 * (t + 1)],
+                            in0=dxb[:, 256 * e : 256 * (e + 1)],
+                            scalar=mkf[:, i : i + 1],
+                            in1=sx_pl,
+                            op0=ALU.mult,
+                            op1=ALU.add,
+                        )
             for v in range(2):
-                y = ep.tile([P, 1024], F32, tag="xf%d" % v, name="y")
-                nc.vector.tensor_tensor(
-                    out=y[:].rearrange("p (n t) -> p n t", t=4),
-                    in0=dx[:].rearrange("p (n t) -> p n t", t=4),
-                    in1=mkf[:, 16 * v + 4 * g : 16 * v + 4 * g + 4].unsqueeze(1).to_broadcast([P, 256, 4]),
-                    op=ALU.mult,
-                )
                 o0 = 4096 * v + 1024 * g
-                nc.vector.tensor_tensor(out=xg[:, o0 : o0 + 1024], in0=y[:], in1=sx_g, op=ALU.add)
+                nc.gpsimd.tensor_scalar(
+                    out=xg[:, o0 : o0 + 1024].rearrange("p (n t) -> p n t", t=4),
+                    in0=plns[v][:].rearrange("p (t n) -> p n t", t=4),
+                    scalar1=1.0,
+                    scalar2=0.0,
+                    op0=ALU.mult,
+                    op1=ALU.add,
+                )
+        load_w(0, 1, 1)
+        load_w(1, 1, 0)
 
         xcodes = const.tile([P, 2048], U32, name="xcodes", align_bytes=64)
         xscl = const.tile([P, 2048], U8, name="xscl", align_bytes=64)
-        for v in range(2):
+
+        def quantise_x(v):
             nc.vector.quantize_mx(
                 out=xcodes[:, 1024 * v : 1024 * (v + 1)].bitcast(FP8X4),
                 scales=xscl[:, 1024 * v : 1024 * (v + 1)],
                 in_=xg[:, 4096 * v : 4096 * (v + 1)],
             )
 
-        tfw = const.tile([P, 4096], F32, name="tfw")
-        nc.scalar.copy(out=tfw[:, 0:2048], in_=tftd[:, 0:2048])
-        nc.scalar.activation(out=tfw[:, 2048:4096], in_=tftd[:, 2048:4096], func=ACT.Exp)
-        tfw_v = tfw[:].rearrange("p (h d) -> p h d", h=2)
-
-        def prep_w(v, j):
-            halves = raw_w[(v, j)]
+        def regroup_w(v, j):
             gt = grp.tile([P, 8192], BF16, tag="grp", name="gt", align_bytes=64)
             gw = gt[:].bitcast(F32).rearrange("p (g d u) -> p g d u", g=4, d=NT, u=2)
-            codes = cod.tile([P, 2048], U32, tag="codes", name="codes", align_bytes=64)
-            scl = cod.tile([P, 2048], U8, tag="scl", name="scl", align_bytes=64)
             for c in range(4):
-                wf = halves[c // 2][:].bitcast(F32)
+                wf = raw_w[(v, j, c // 2)][:].bitcast(F32)
                 base = 1024 * (c % 2)
                 for hb in range(2):
                     bank = tp.tile([P, 512], F32, tag="tp", name="bank")
@@ -183,6 +190,11 @@ def tile_rwkv_timemix_for_quant_pa_kernel(
                         out=gw[:, 2 * hb : 2 * hb + 2, 128 * c : 128 * (c + 1), :],
                         in_=bank[:].rearrange("p (g u d) -> p g d u", g=2, u=2, d=128),
                     )
+            return gt
+
+        def quantise_w(gt):
+            codes = cod.tile([P, 2048], U32, tag="codes", name="codes", align_bytes=64)
+            scl = cod.tile([P, 2048], U8, tag="scl", name="scl", align_bytes=64)
             for hb in range(2):
                 nc.vector.quantize_mx(
                     out=codes[:, 1024 * hb : 1024 * (hb + 1)].bitcast(FP8X4),
@@ -191,97 +203,143 @@ def tile_rwkv_timemix_for_quant_pa_kernel(
                 )
             return codes, scl
 
-        def project(wq, r):
-            banks = []
-            for v in range(2):
-                codes, scl = wq[v]
-                ps = acc.tile([P, NT], F32, tag="acc", name="ps")
-                for g in range(4):
-                    c0 = 1024 * v + 256 * g + 128 * r
-                    nc.tensor.matmul_mx(
-                        out=ps[:],
-                        lhsT=xcodes[:, c0 : c0 + 128].bitcast(FP8X4),
-                        lhsT_scale=xscl[:, c0 : c0 + 128],
-                        rhs=codes[:, NT * g : NT * (g + 1)].bitcast(FP8X4),
-                        rhs_scale=scl[:, NT * g : NT * (g + 1)],
-                        start=(g == 0),
-                        stop=(g == 3),
-                    )
-                banks.append(ps)
-            return banks
+        def project(v, wq, r):
+            codes, scl = wq
+            ps = acc.tile([P, NT], F32, tag="acc", name="ps")
+            for g in range(4):
+                c0 = 1024 * v + 256 * g + 128 * r
+                nc.tensor.matmul_mx(
+                    out=ps[:],
+                    lhsT=xcodes[:, c0 : c0 + 128].bitcast(FP8X4),
+                    lhsT_scale=xscl[:, c0 : c0 + 128],
+                    rhs=codes[:, NT * g : NT * (g + 1)].bitcast(FP8X4),
+                    rhs_scale=scl[:, NT * g : NT * (g + 1)],
+                    start=(g == 0),
+                    stop=(g == 3),
+                )
+            return ps
 
-        def front(j, r, k_ps):
+        tfw = const.tile([P, 4096], F32, name="tfw")
+        tfw_v = tfw[:].rearrange("p (h d) -> p h d", h=2)
+
+        def spread_vectors(lo, hi):
+            nc.scalar.copy(out=tfw[:, lo:hi], in_=tftd[:, lo:hi])
+            nc.scalar.activation(out=tfw[:, 2048 + lo : 2048 + hi], in_=tftd[:, 2048 + lo : 2048 + hi], func=ACT.Exp)
+
+        two = "p (h d) -> p h d"
+
+        def store(dst, j, r, src):
+            nc.sync.dma_start(out=dst[P * r : P * (r + 1), NT * j : NT * (j + 1)], in_=src)
+
+        def per_row_tile(t, r):
+            return t[:, NT * r : NT * (r + 1)]
+
+        def twice(ap):
+            return ap.unsqueeze(1).to_broadcast([P, 2, NT])
+
+        def exponents(j, k_ps):
             sp_t = states[j][0]
-            nq = ep.tile([P, NT], F32, tag="nq", name="nq")
-            nc.vector.tensor_tensor(out=nq[:], in0=sp_t[:, NT * r : NT * (r + 1)], in1=k_ps[:], op=ALU.subtract)
-            ndd = ep.tile([P, 1024], F32, tag="ndd", name="ndd")
-            nc.vector.tensor_tensor(
-                out=ndd[:].rearrange("p (h d) -> p h d", h=2),
-                in0=nq[:].unsqueeze(1).to_broadcast([P, 2, NT]),
-                in1=tfw_v[:, :, NT * j : NT * (j + 1)],
-                op=ALU.subtract,
-            )
-            p2 = ep.tile([P, NT], F32, tag="p2", name="p2")
-            nc.vector.scalar_tensor_tensor(
-                out=p2[:], in0=ndd[:, NT : 2 * NT], scalar=0.0, in1=k_ps[:], op0=ALU.max, op1=ALU.add
-            )
-            nc.gpsimd.dma_start(out=out_4[P * r : P * (r + 1), NT * j : NT * (j + 1)], in_=p2[:])
-            xf1 = ep.tile([P, 1024], F32, tag="xf0", name="xf1")
-            nc.scalar.activation(out=xf1[:], in_=ndd[:], func=ACT.Exp)
-            xf2 = ep.tile([P, 1024], F32, tag="xf1", name="xf2")
-            nc.scalar.activation(out=xf2[:], in_=ndd[:], func=ACT.Exp, scale=-1.0)
+            nq = [ep.tile([P, NT], F32, tag="nq", name="nq") for r in range(2)]
+            ndd = [ep.tile([P, 1024], F32, tag="ndd", name="ndd") for r in range(2)]
+            xf1 = [ep.tile([P, 1024], F32, tag="xf0", name="xf1") for r in range(2)]
+            xf2 = [ep.tile([P, 1024], F32, tag="xf1", name="xf2") for r in range(2)]
+            p2 = [ep.tile([P, NT], F32, tag="p2", name="p2") for r in range(2)]
+            for r in range(2):
+                nc.vector.tensor_tensor(out=nq[r][:], in0=per_row_tile(sp_t, r), in1=k_ps[r][:], op=ALU.subtract)
+            for r in range(2):
+                nc.vector.tensor_tensor(
+                    out=ndd[r][:].rearrange(two, h=2),
+                    in0=twice(nq[r][:]),
+                    in1=tfw_v[:, :, NT * j : NT * (j + 1)],
+                    op=ALU.subtract,
+                )
+            for r in range(2):
+                nc.scalar.activation(out=xf1[r][:], in_=ndd[r][:], func=ACT.Exp)
+            for r in range(2):
+                nc.scalar.activation(out=xf2[r][:], in_=ndd[r][:], func=ACT.Exp, scale=-1.0)
+            for r in range(2):
+                nc.vector.scalar_tensor_tensor(
+                    out=p2[r][:], in0=ndd[r][:, NT : 2 * NT], scalar=0.0, in1=k_ps[r][:], op0=ALU.max, op1=ALU.add
+                )
+                store(out_4, j, r, p2[r][:])
             return xf1, xf2
 
-        def back(j, r, v_ps, xf1, xf2):
+        def numerators(j, v_ps, xf1, xf2):
             a_t = states[j][1]
-            b_t = states[j][2]
-            two = "p (h d) -> p h d"
-            t1 = ep.tile([P, 1024], F32, tag="t1", name="t1")
-            nc.vector.scalar_tensor_tensor(
-                out=t1[:].rearrange(two, h=2),
-                in0=xf1[:].rearrange(two, h=2),
-                scalar=1.0,
-                in1=a_t[:, NT * r : NT * (r + 1)].unsqueeze(1).to_broadcast([P, 2, NT]),
-                op0=ALU.min,
-                op1=ALU.mult,
-            )
-            t2 = ep.tile([P, 1024], F32, tag="t2", name="t2")
-            nc.vector.scalar_tensor_tensor(
-                out=t2[:].rearrange(two, h=2),
-                in0=xf2[:].rearrange(two, h=2),
-                scalar=1.0,
-                in1=v_ps[:].unsqueeze(1).to_broadcast([P, 2, NT]),
-                op0=ALU.min,
-                op1=ALU.mult,
-            )
-            nc.vector.tensor_tensor(out=t1[:], in0=t1[:], in1=t2[:], op=ALU.add)
-            rows = slice(P * r, P * (r + 1))
-            cols = slice(NT * j, NT * (j + 1))
-            nc.gpsimd.dma_start(out=out_0[rows, cols], in_=t1[:, 0:NT])
-            nc.gpsimd.dma_start(out=out_2[rows, cols], in_=t1[:, NT : 2 * NT])
-            nc.vector.scalar_tensor_tensor(
-                out=xf1[:].rearrange(two, h=2),
-                in0=xf1[:].rearrange(two, h=2),
-                scalar=1.0,
-                in1=b_t[:, NT * r : NT * (r + 1)].unsqueeze(1).to_broadcast([P, 2, NT]),
-                op0=ALU.min,
-                op1=ALU.mult,
-            )
-            nc.vector.scalar_tensor_tensor(
-                out=xf2[:], in0=xf2[:], scalar=1.0, in1=xf1[:], op0=ALU.min, op1=ALU.add
-            )
-            nc.gpsimd.dma_start(out=out_1[rows, cols], in_=xf2[:, 0:NT])
-            nc.gpsimd.dma_start(out=out_3[rows, cols], in_=xf2[:, NT : 2 * NT])
-
-        wq = (prep_w(0, 0), prep_w(1, 0))
-        for j in range(4):
-            if j + 1 < 4:
-                raw_w[(0, j + 1)] = load_w(0, j + 1)
-                raw_w[(1, j + 1)] = load_w(1, j + 1)
-                states[j + 1] = load_states(j + 1)
-            banks = [project(wq, r) for r in range(2)]
-            exps = [front(j, r, banks[r][0]) for r in range(2)]
-            if j + 1 < 4:
-                wq = (prep_w(0, j + 1), prep_w(1, j + 1))
+            t1 = [ep.tile([P, 1024], F32, tag="t1", name="t1") for r in range(2)]
+            t2 = [ep.tile([P, 1024], F32, tag="t2", name="t2") for r in range(2)]
             for r in range(2):
-                back(j, r, banks[r][1], exps[r][0], exps[r][1])
+                nc.vector.scalar_tensor_tensor(
+                    out=t1[r][:].rearrange(two, h=2),
+                    in0=xf1[r][:].rearrange(two, h=2),
+                    scalar=1.0,
+                    in1=twice(per_row_tile(a_t, r)),
+                    op0=ALU.min,
+                    op1=ALU.mult,
+                )
+            for r in range(2):
+                nc.vector.scalar_tensor_tensor(
+                    out=t2[r][:].rearrange(two, h=2),
+                    in0=xf2[r][:].rearrange(two, h=2),
+                    scalar=1.0,
+                    in1=twice(v_ps[r][:]),
+                    op0=ALU.min,
+                    op1=ALU.mult,
+                )
+            for r in range(2):
+                nc.vector.tensor_tensor(out=t1[r][:], in0=t1[r][:], in1=t2[r][:], op=ALU.add)
+                store(out_0, j, r, t1[r][:, 0:NT])
+                store(out_2, j, r, t1[r][:, NT : 2 * NT])
+
+        def denominators(j, xf1, xf2):
+            b_t = states[j][2]
+            for r in range(2):
+                nc.vector.scalar_tensor_tensor(
+                    out=xf1[r][:].rearrange(two, h=2),
+                    in0=xf1[r][:].rearrange(two, h=2),
+                    scalar=1.0,
+                    in1=twice(per_row_tile(b_t, r)),
+                    op0=ALU.min,
+                    op1=ALU.mult,
+                )
+            for r in range(2):
+                nc.vector.scalar_tensor_tensor(
+                    out=xf2[r][:], in0=xf2[r][:], scalar=1.0, in1=xf1[r][:], op0=ALU.min, op1=ALU.add
+                )
+                store(out_1, j, r, xf2[r][:, 0:NT])
+                store(out_3, j, r, xf2[r][:, NT : 2 * NT])
+
+        gt_k = regroup_w(0, 0)
+        load_w(1, 1, 1)
+        load_states(1)
+        wq_k = quantise_w(gt_k)
+        quantise_x(0)
+        gt_v = regroup_w(1, 0)
+        spread_vectors(0, NT)
+        wq_v = quantise_w(gt_v)
+        quantise_x(1)
+        k_ps = [project(0, wq_k, r) for r in range(2)]
+        v_ps = [project(1, wq_v, r) for r in range(2)]
+
+        for j in range(TILES):
+            xf1, xf2 = exponents(j, k_ps)
+            if j == 0:
+                spread_vectors(NT, D)
+            if j + 2 < TILES:
+                load_w(0, j + 2, 0)
+                load_w(0, j + 2, 1)
+            if j + 1 < TILES:
+                gt_k = regroup_w(0, j + 1)
+                gt_v = regroup_w(1, j + 1)
+            numerators(j, v_ps, xf1, xf2)
+            if j + 2 < TILES:
+                load_w(1, j + 2, 0)
+                load_w(1, j + 2, 1)
+            denominators(j, xf1, xf2)
+            if j + 2 < TILES:
+                load_states(j + 2)
+            if j + 1 < TILES:
+                wq_k = quantise_w(gt_k)
+                wq_v = quantise_w(gt_v)
+                k_ps = [project(0, wq_k, r) for r in range(2)]
+                v_ps = [project(1, wq_v, r) for r in range(2)]

@@ -17,6 +17,7 @@ E = 2048
 D = 2048
 NT = 512
 TILES = D // NT
+AHEAD = 4
 FLOPS = 2 * 2 * ROWS * E * D
 
 
@@ -75,16 +76,12 @@ def tile_rwkv_timemix_for_quant_pa_kernel(
                 tiles.append(t)
             states[j] = tiles
 
-        mkb = const.tile([P, 32], BF16, name="mkb")
-        with nc.allow_non_contiguous_dma(reason="mix coefficients, two neighbouring k to a partition"):
-            nc.sync.dma_start(
-                out=mkb[:, 0:16].rearrange("p (a e) -> p a e", e=2),
-                in_=time_mix_k.rearrange("o (a p e) -> p (o a) e", a=8, p=P, e=2),
-            )
-            nc.sync.dma_start(
-                out=mkb[:, 16:32].rearrange("p (a e) -> p a e", e=2),
-                in_=time_mix_v.rearrange("o (a p e) -> p (o a) e", a=8, p=P, e=2),
-            )
+        mraw = const.tile([P, 256], BF16, name="mraw")
+        nc.vector.memset(mraw[:], 0.0)
+        warm_in = const.tile([P, 1], F32, name="warm_in")
+        warm_out = const.tile([P, 1], F32, name="warm_out")
+        nc.vector.memset(warm_in[:], 0.0)
+        nc.scalar.activation(out=warm_out[:], in_=warm_in[:], func=ACT.Exp)
         x_sb = ring.tile([P, 4096], BF16, tag="ring", name="x_sb")
         sx_sb = ring.tile([P, 4096], BF16, tag="ring", name="sx_sb")
         for g in range(4):
@@ -93,6 +90,9 @@ def tile_rwkv_timemix_for_quant_pa_kernel(
                     out=dst[:, 1024 * g : 1024 * (g + 1)].rearrange("p (r k) -> p r k", r=2),
                     in_=src.rearrange("(r p) k -> p r k", p=P)[:, :, 512 * g : 512 * (g + 1)],
                 )
+            if g == 0:
+                nc.sync.dma_start(out=mraw[0:8, :], in_=time_mix_k.rearrange("o (a c) -> (o a) c", a=8))
+                nc.sync.dma_start(out=mraw[8:16, :], in_=time_mix_v.rearrange("o (a c) -> (o a) c", a=8))
         for v in range(2):
             for h in range(2):
                 load_w(v, 0, h)
@@ -108,12 +108,10 @@ def tile_rwkv_timemix_for_quant_pa_kernel(
         make_identity(nc, identb[:])
         nidentb = const.tile([P, P], BF16, name="nidentb")
         nc.vector.tensor_scalar_mul(out=nidentb[:], in0=identb[:], scalar1=-1.0)
-        warm_in = const.tile([P, 1], F32, name="warm_in")
-        warm_out = const.tile([P, 1], F32, name="warm_out")
-        nc.vector.memset(warm_in[:], 0.0)
-        nc.scalar.activation(out=warm_out[:], in_=warm_in[:], func=ACT.Exp)
+        mkt = tp.tile([P, 512], F32, tag="tp", name="mkt")
+        nc.tensor.transpose(mkt[:, 0:128], mraw[:].bitcast(F32), ident[:])
         mkf = const.tile([P, 32], F32, name="mkf")
-        nc.vector.tensor_copy(out=mkf[:], in_=mkb[:])
+        nc.vector.tensor_copy(out=mkf[:], in_=mkt[:, 0:16].bitcast(BF16))
 
         xg = grp.tile([P, 8192], BF16, tag="grp", name="xg", align_bytes=64)
         sw = sx_sb[:].bitcast(F32)
@@ -173,26 +171,30 @@ def tile_rwkv_timemix_for_quant_pa_kernel(
                 in_=xg[:, 4096 * v : 4096 * (v + 1)],
             )
 
-        def regroup_w(v, j):
-            gt = grp.tile([P, 8192], BF16, tag="grp", name="gt", align_bytes=64)
-            gw = gt[:].bitcast(F32).rearrange("p (g d u) -> p g d u", g=4, d=NT, u=2)
-            for c in range(4):
-                wf = raw_w[(v, j, c // 2)][:].bitcast(F32)
-                base = 1024 * (c % 2)
-                for hb in range(2):
-                    bank = tp.tile([P, 512], F32, tag="tp", name="bank")
-                    for gi in range(2):
-                        for u in range(2):
-                            src = base + 256 * (2 * hb + gi) + 128 * u
-                            col = 128 * (2 * gi + u)
-                            nc.tensor.transpose(bank[:, col : col + 128], wf[:, src : src + 128], ident[:])
-                    nc.scalar.copy(
-                        out=gw[:, 2 * hb : 2 * hb + 2, 128 * c : 128 * (c + 1), :],
-                        in_=bank[:].rearrange("p (g u d) -> p g d u", g=2, u=2, d=128),
-                    )
-            return gt
+        bank_jobs = [(j, v, c, hb) for j in range(TILES) for v in range(2) for c in range(4) for hb in range(2)]
+        banks_done = [0]
+        grouped = {}
 
-        def quantise_w(gt):
+        def regroup_banks(count):
+            for j, v, c, hb in bank_jobs[banks_done[0] : banks_done[0] + count]:
+                if c == 0 and hb == 0:
+                    grouped[(v, j)] = grp.tile([P, 8192], BF16, tag="grp", name="gt", align_bytes=64)
+                gw = grouped[(v, j)][:].bitcast(F32).rearrange("p (g d u) -> p g d u", g=4, d=NT, u=2)
+                wf = raw_w[(v, j, c // 2)][:].bitcast(F32)
+                bank = tp.tile([P, 512], F32, tag="tp", name="bank")
+                for gi in range(2):
+                    for u in range(2):
+                        src = 1024 * (c % 2) + 256 * (2 * hb + gi) + 128 * u
+                        col = 128 * (2 * gi + u)
+                        nc.tensor.transpose(bank[:, col : col + 128], wf[:, src : src + 128], ident[:])
+                nc.scalar.copy(
+                    out=gw[:, 2 * hb : 2 * hb + 2, 128 * c : 128 * (c + 1), :],
+                    in_=bank[:].rearrange("p (g u d) -> p g d u", g=2, u=2, d=128),
+                )
+            banks_done[0] += count
+
+        def quantise_w(v, j):
+            gt = grouped[(v, j)]
             codes = cod.tile([P, 2048], U32, tag="codes", name="codes", align_bytes=64)
             scl = cod.tile([P, 2048], U8, tag="scl", name="scl", align_bytes=64)
             for hb in range(2):
@@ -309,14 +311,15 @@ def tile_rwkv_timemix_for_quant_pa_kernel(
                 store(out_1, j, r, xf2[r][:, 0:NT])
                 store(out_3, j, r, xf2[r][:, NT : 2 * NT])
 
-        gt_k = regroup_w(0, 0)
+        regroup_banks(8)
         load_w(1, 1, 1)
         load_states(1)
-        wq_k = quantise_w(gt_k)
+        wq_k = quantise_w(0, 0)
         quantise_x(0)
-        gt_v = regroup_w(1, 0)
+        regroup_banks(8)
         spread_vectors(0, NT)
-        wq_v = quantise_w(gt_v)
+        regroup_banks(AHEAD)
+        wq_v = quantise_w(1, 0)
         quantise_x(1)
         k_ps = [project(0, wq_k, r) for r in range(2)]
         v_ps = [project(1, wq_v, r) for r in range(2)]
@@ -329,8 +332,7 @@ def tile_rwkv_timemix_for_quant_pa_kernel(
                 load_w(0, j + 2, 0)
                 load_w(0, j + 2, 1)
             if j + 1 < TILES:
-                gt_k = regroup_w(0, j + 1)
-                gt_v = regroup_w(1, j + 1)
+                regroup_banks(16 - AHEAD)
             numerators(j, v_ps, xf1, xf2)
             if j + 2 < TILES:
                 load_w(1, j + 2, 0)
@@ -338,8 +340,9 @@ def tile_rwkv_timemix_for_quant_pa_kernel(
             denominators(j, xf1, xf2)
             if j + 2 < TILES:
                 load_states(j + 2)
+                regroup_banks(AHEAD)
             if j + 1 < TILES:
-                wq_k = quantise_w(gt_k)
-                wq_v = quantise_w(gt_v)
+                wq_k = quantise_w(0, j + 1)
+                wq_v = quantise_w(1, j + 1)
                 k_ps = [project(0, wq_k, r) for r in range(2)]
                 v_ps = [project(1, wq_v, r) for r in range(2)]

@@ -17,7 +17,6 @@ E = 2048
 D = 2048
 NT = 512
 TILES = D // NT
-AHEAD = 4
 FLOPS = 2 * 2 * ROWS * E * D
 
 
@@ -76,12 +75,16 @@ def tile_rwkv_timemix_for_quant_pa_kernel(
                 tiles.append(t)
             states[j] = tiles
 
-        mraw = const.tile([P, 256], BF16, name="mraw")
-        nc.vector.memset(mraw[:], 0.0)
-        warm_in = const.tile([P, 1], F32, name="warm_in")
-        warm_out = const.tile([P, 1], F32, name="warm_out")
-        nc.vector.memset(warm_in[:], 0.0)
-        nc.scalar.activation(out=warm_out[:], in_=warm_in[:], func=ACT.Exp)
+        mkb = const.tile([P, 32], BF16, name="mkb")
+        with nc.allow_non_contiguous_dma(reason="mix coefficients, two neighbouring k to a partition"):
+            nc.sync.dma_start(
+                out=mkb[:, 0:16].rearrange("p (a e) -> p a e", e=2),
+                in_=time_mix_k.rearrange("o (a p e) -> p (o a) e", a=8, p=P, e=2),
+            )
+            nc.sync.dma_start(
+                out=mkb[:, 16:32].rearrange("p (a e) -> p a e", e=2),
+                in_=time_mix_v.rearrange("o (a p e) -> p (o a) e", a=8, p=P, e=2),
+            )
         x_sb = ring.tile([P, 4096], BF16, tag="ring", name="x_sb")
         sx_sb = ring.tile([P, 4096], BF16, tag="ring", name="sx_sb")
         for g in range(4):
@@ -90,9 +93,6 @@ def tile_rwkv_timemix_for_quant_pa_kernel(
                     out=dst[:, 1024 * g : 1024 * (g + 1)].rearrange("p (r k) -> p r k", r=2),
                     in_=src.rearrange("(r p) k -> p r k", p=P)[:, :, 512 * g : 512 * (g + 1)],
                 )
-            if g == 0:
-                nc.sync.dma_start(out=mraw[0:8, :], in_=time_mix_k.rearrange("o (a c) -> (o a) c", a=8))
-                nc.sync.dma_start(out=mraw[8:16, :], in_=time_mix_v.rearrange("o (a c) -> (o a) c", a=8))
         for v in range(2):
             for h in range(2):
                 load_w(v, 0, h)
@@ -108,10 +108,12 @@ def tile_rwkv_timemix_for_quant_pa_kernel(
         make_identity(nc, identb[:])
         nidentb = const.tile([P, P], BF16, name="nidentb")
         nc.vector.tensor_scalar_mul(out=nidentb[:], in0=identb[:], scalar1=-1.0)
-        mkt = tp.tile([P, 512], F32, tag="tp", name="mkt")
-        nc.tensor.transpose(mkt[:, 0:128], mraw[:].bitcast(F32), ident[:])
+        warm_in = const.tile([P, 1], F32, name="warm_in")
+        warm_out = const.tile([P, 1], F32, name="warm_out")
+        nc.vector.memset(warm_in[:], 0.0)
+        nc.scalar.activation(out=warm_out[:], in_=warm_in[:], func=ACT.Exp)
         mkf = const.tile([P, 32], F32, name="mkf")
-        nc.vector.tensor_copy(out=mkf[:], in_=mkt[:, 0:16].bitcast(BF16))
+        nc.vector.tensor_copy(out=mkf[:], in_=mkb[:])
 
         xg = grp.tile([P, 8192], BF16, tag="grp", name="xg", align_bytes=64)
         sw = sx_sb[:].bitcast(F32)
@@ -126,7 +128,7 @@ def tile_rwkv_timemix_for_quant_pa_kernel(
             nc.scalar.copy(out=sxs[:].bitcast(F32), in_=sb[:])
             plns = [ep.tile([P, 1024], BF16, tag="t%d" % (v + 1), name="pln") for v in range(2)]
             for u in range(2):
-                dxb = tp.tile([P, 512], F32, tag="tp", name="dxb")
+                dxb = acc.tile([P, 512], F32, tag="acc", name="dxb")
                 for e in range(2):
                     for r in range(2):
                         base = 1024 * g + 512 * r + 256 * u
@@ -171,30 +173,26 @@ def tile_rwkv_timemix_for_quant_pa_kernel(
                 in_=xg[:, 4096 * v : 4096 * (v + 1)],
             )
 
-        bank_jobs = [(j, v, c, hb) for j in range(TILES) for v in range(2) for c in range(4) for hb in range(2)]
-        banks_done = [0]
-        grouped = {}
-
-        def regroup_banks(count):
-            for j, v, c, hb in bank_jobs[banks_done[0] : banks_done[0] + count]:
-                if c == 0 and hb == 0:
-                    grouped[(v, j)] = grp.tile([P, 8192], BF16, tag="grp", name="gt", align_bytes=64)
-                gw = grouped[(v, j)][:].bitcast(F32).rearrange("p (g d u) -> p g d u", g=4, d=NT, u=2)
+        def regroup_w(v, j):
+            gt = grp.tile([P, 8192], BF16, tag="grp", name="gt", align_bytes=64)
+            gw = gt[:].bitcast(F32).rearrange("p (g d u) -> p g d u", g=4, d=NT, u=2)
+            for c in range(4):
                 wf = raw_w[(v, j, c // 2)][:].bitcast(F32)
-                bank = tp.tile([P, 512], F32, tag="tp", name="bank")
-                for gi in range(2):
-                    for u in range(2):
-                        src = 1024 * (c % 2) + 256 * (2 * hb + gi) + 128 * u
-                        col = 128 * (2 * gi + u)
-                        nc.tensor.transpose(bank[:, col : col + 128], wf[:, src : src + 128], ident[:])
-                nc.scalar.copy(
-                    out=gw[:, 2 * hb : 2 * hb + 2, 128 * c : 128 * (c + 1), :],
-                    in_=bank[:].rearrange("p (g u d) -> p g d u", g=2, u=2, d=128),
-                )
-            banks_done[0] += count
+                base = 1024 * (c % 2)
+                for hb in range(2):
+                    bank = tp.tile([P, 512], F32, tag="tp", name="bank")
+                    for gi in range(2):
+                        for u in range(2):
+                            src = base + 256 * (2 * hb + gi) + 128 * u
+                            col = 128 * (2 * gi + u)
+                            nc.tensor.transpose(bank[:, col : col + 128], wf[:, src : src + 128], ident[:])
+                    nc.scalar.copy(
+                        out=gw[:, 2 * hb : 2 * hb + 2, 128 * c : 128 * (c + 1), :],
+                        in_=bank[:].rearrange("p (g u d) -> p g d u", g=2, u=2, d=128),
+                    )
+            return gt
 
-        def quantise_w(v, j):
-            gt = grouped[(v, j)]
+        def quantise_w(gt):
             codes = cod.tile([P, 2048], U32, tag="codes", name="codes", align_bytes=64)
             scl = cod.tile([P, 2048], U8, tag="scl", name="scl", align_bytes=64)
             for hb in range(2):
@@ -311,15 +309,14 @@ def tile_rwkv_timemix_for_quant_pa_kernel(
                 store(out_1, j, r, xf2[r][:, 0:NT])
                 store(out_3, j, r, xf2[r][:, NT : 2 * NT])
 
-        regroup_banks(8)
+        gt_k = regroup_w(0, 0)
         load_w(1, 1, 1)
         load_states(1)
-        wq_k = quantise_w(0, 0)
+        wq_k = quantise_w(gt_k)
         quantise_x(0)
-        regroup_banks(8)
+        gt_v = regroup_w(1, 0)
         spread_vectors(0, NT)
-        regroup_banks(AHEAD)
-        wq_v = quantise_w(1, 0)
+        wq_v = quantise_w(gt_v)
         quantise_x(1)
         k_ps = [project(0, wq_k, r) for r in range(2)]
         v_ps = [project(1, wq_v, r) for r in range(2)]
@@ -332,7 +329,8 @@ def tile_rwkv_timemix_for_quant_pa_kernel(
                 load_w(0, j + 2, 0)
                 load_w(0, j + 2, 1)
             if j + 1 < TILES:
-                regroup_banks(16 - AHEAD)
+                gt_k = regroup_w(0, j + 1)
+                gt_v = regroup_w(1, j + 1)
             numerators(j, v_ps, xf1, xf2)
             if j + 2 < TILES:
                 load_w(1, j + 2, 0)
@@ -340,9 +338,8 @@ def tile_rwkv_timemix_for_quant_pa_kernel(
             denominators(j, xf1, xf2)
             if j + 2 < TILES:
                 load_states(j + 2)
-                regroup_banks(AHEAD)
             if j + 1 < TILES:
-                wq_k = quantise_w(0, j + 1)
-                wq_v = quantise_w(1, j + 1)
+                wq_k = quantise_w(gt_k)
+                wq_v = quantise_w(gt_v)
                 k_ps = [project(0, wq_k, r) for r in range(2)]
                 v_ps = [project(1, wq_v, r) for r in range(2)]

@@ -291,7 +291,7 @@ def tile_rwkv_timemix_for_quant_pa_kernel(
                 store(out_0, j, r, t1[r][:, 0:NT])
                 store(out_2, j, r, t1[r][:, NT : 2 * NT])
 
-        def denominators(j, xf1, xf2):
+        def weighted_b(j, xf1):
             b_t = states[j][2]
             for r in range(2):
                 nc.vector.scalar_tensor_tensor(
@@ -302,6 +302,8 @@ def tile_rwkv_timemix_for_quant_pa_kernel(
                     op0=ALU.min,
                     op1=ALU.mult,
                 )
+
+        def denominators(j, xf1, xf2):
             for r in range(2):
                 nc.vector.scalar_tensor_tensor(
                     out=xf2[r][:], in0=xf2[r][:], scalar=1.0, in1=xf1[r][:], op0=ALU.min, op1=ALU.add
@@ -335,11 +337,13 @@ def tile_rwkv_timemix_for_quant_pa_kernel(
             if j + 2 < TILES:
                 load_w(1, j + 2, 0)
                 load_w(1, j + 2, 1)
+            weighted_b(j, xf1)
+            if j + 1 < TILES:
+                wq_k = quantise_w(gt_k)
             denominators(j, xf1, xf2)
             if j + 2 < TILES:
                 load_states(j + 2)
             if j + 1 < TILES:
-                wq_k = quantise_w(gt_k)
                 wq_v = quantise_w(gt_v)
                 k_ps = [project(0, wq_k, r) for r in range(2)]
                 v_ps = [project(1, wq_v, r) for r in range(2)]

@@ -77,14 +77,18 @@ def tile_rwkv_timemix_for_quant_pa_kernel(
 
         mkb = const.tile([P, 32], BF16, name="mkb")
         with nc.allow_non_contiguous_dma(reason="mix coefficients, two neighbouring k to a partition"):
-            nc.sync.dma_start(
+            nc.scalar.dma_start(
                 out=mkb[:, 0:16].rearrange("p (a e) -> p a e", e=2),
                 in_=time_mix_k.rearrange("o (a p e) -> p (o a) e", a=8, p=P, e=2),
             )
-            nc.sync.dma_start(
+            nc.scalar.dma_start(
                 out=mkb[:, 16:32].rearrange("p (a e) -> p a e", e=2),
                 in_=time_mix_v.rearrange("o (a p e) -> p (o a) e", a=8, p=P, e=2),
             )
+        vec_rows = const.tile([P, D], BF16, name="vec_rows")
+        nc.vector.memset(vec_rows[:], 0.0)
+        nc.scalar.dma_start(out=vec_rows[0:1, :], in_=time_first.unsqueeze(0))
+        nc.scalar.dma_start(out=vec_rows[1:2, :], in_=time_decay.unsqueeze(0))
         x_sb = ring.tile([P, 4096], BF16, tag="ring", name="x_sb")
         sx_sb = ring.tile([P, 4096], BF16, tag="ring", name="sx_sb")
         for g in range(4):
@@ -96,11 +100,9 @@ def tile_rwkv_timemix_for_quant_pa_kernel(
         for v in range(2):
             for h in range(2):
                 load_w(v, 0, h)
-        tftd = ring.tile([P, 4096], BF16, tag="ring", name="tftd")
-        nc.sync.dma_start(out=tftd[:, 0:2048], in_=time_first.partition_broadcast(P))
-        nc.sync.dma_start(out=tftd[:, 2048:4096], in_=time_decay.partition_broadcast(P))
         load_states(0)
         load_w(0, 1, 0)
+        load_w(0, 1, 1)
 
         ident = const.tile([P, P], F32, name="ident")
         make_identity(nc, ident[:])
@@ -160,8 +162,8 @@ def tile_rwkv_timemix_for_quant_pa_kernel(
                     op0=ALU.mult,
                     op1=ALU.add,
                 )
-        load_w(0, 1, 1)
         load_w(1, 1, 0)
+        load_w(1, 1, 1)
 
         xcodes = const.tile([P, 2048], U32, name="xcodes", align_bytes=64)
         xscl = const.tile([P, 2048], U8, name="xscl", align_bytes=64)
@@ -222,9 +224,21 @@ def tile_rwkv_timemix_for_quant_pa_kernel(
         tfw = const.tile([P, 4096], F32, name="tfw")
         tfw_v = tfw[:].rearrange("p (h d) -> p h d", h=2)
 
-        def spread_vectors(lo, hi):
-            nc.scalar.copy(out=tfw[:, lo:hi], in_=tftd[:, lo:hi])
-            nc.scalar.activation(out=tfw[:, 2048 + lo : 2048 + hi], in_=tftd[:, 2048 + lo : 2048 + hi], func=ACT.Exp)
+        def spread_vectors(j):
+            cols = slice(NT * j, NT * (j + 1))
+            spread = []
+            for row in range(2):
+                ps = tp.tile([P, NT], F32, tag="tp", name="spread_ps")
+                nc.tensor.matmul(
+                    out=ps[:],
+                    lhsT=identb[:, row : row + 1].to_broadcast([P, P]),
+                    rhs=vec_rows[:, cols],
+                    start=True,
+                    stop=True,
+                )
+                spread.append(ps)
+            nc.scalar.copy(out=tfw[:, NT * j : NT * (j + 1)], in_=spread[0][:])
+            nc.scalar.activation(out=tfw[:, D + NT * j : D + NT * (j + 1)], in_=spread[1][:], func=ACT.Exp)
 
         two = "p (h d) -> p h d"
 
@@ -291,7 +305,7 @@ def tile_rwkv_timemix_for_quant_pa_kernel(
                 store(out_0, j, r, t1[r][:, 0:NT])
                 store(out_2, j, r, t1[r][:, NT : 2 * NT])
 
-        def weighted_b(j, xf1):
+        def denominators(j, xf1, xf2):
             b_t = states[j][2]
             for r in range(2):
                 nc.vector.scalar_tensor_tensor(
@@ -302,8 +316,6 @@ def tile_rwkv_timemix_for_quant_pa_kernel(
                     op0=ALU.min,
                     op1=ALU.mult,
                 )
-
-        def denominators(j, xf1, xf2):
             for r in range(2):
                 nc.vector.scalar_tensor_tensor(
                     out=xf2[r][:], in0=xf2[r][:], scalar=1.0, in1=xf1[r][:], op0=ALU.min, op1=ALU.add
@@ -312,12 +324,11 @@ def tile_rwkv_timemix_for_quant_pa_kernel(
                 store(out_3, j, r, xf2[r][:, NT : 2 * NT])
 
         gt_k = regroup_w(0, 0)
-        load_w(1, 1, 1)
         load_states(1)
+        spread_vectors(0)
         wq_k = quantise_w(gt_k)
         quantise_x(0)
         gt_v = regroup_w(1, 0)
-        spread_vectors(0, NT)
         wq_v = quantise_w(gt_v)
         quantise_x(1)
         k_ps = [project(0, wq_k, r) for r in range(2)]
@@ -325,8 +336,8 @@ def tile_rwkv_timemix_for_quant_pa_kernel(
 
         for j in range(TILES):
             xf1, xf2 = exponents(j, k_ps)
-            if j == 0:
-                spread_vectors(NT, D)
+            if j + 1 < TILES:
+                spread_vectors(j + 1)
             if j + 2 < TILES:
                 load_w(0, j + 2, 0)
                 load_w(0, j + 2, 1)
@@ -337,13 +348,11 @@ def tile_rwkv_timemix_for_quant_pa_kernel(
             if j + 2 < TILES:
                 load_w(1, j + 2, 0)
                 load_w(1, j + 2, 1)
-            weighted_b(j, xf1)
-            if j + 1 < TILES:
-                wq_k = quantise_w(gt_k)
             denominators(j, xf1, xf2)
             if j + 2 < TILES:
                 load_states(j + 2)
             if j + 1 < TILES:
+                wq_k = quantise_w(gt_k)
                 wq_v = quantise_w(gt_v)
                 k_ps = [project(0, wq_k, r) for r in range(2)]
                 v_ps = [project(1, wq_v, r) for r in range(2)]

from contextlib import ExitStack

import concourse.mybir as mybir
from concourse.masks import make_identity

F32 = mybir.dt.float32
BF16 = mybir.dt.bfloat16
U32 = mybir.dt.uint32
U8 = mybir.dt.uint8
FP8X4 = mybir.dt.float8_e4m3fn_x4
ALU = mybir.AluOpType
ACT = mybir.ActivationFunctionType

P = 128
ROWS = 256
E = 2048
D = 2048
NT = 512
TILES = D // NT
FLOPS = 2 * 2 * ROWS * E * D


def tile_rwkv_timemix_for_quant_pa_kernel(
    tc,
    x,
    state_A,
    state_B,
    state_p,
    state_x,
    time_decay,
    time_first,
    time_mix_k,
    time_mix_v,
    W_key,
    W_value,
    out_0,
    out_1,
    out_2,
    out_3,
    out_4,
):
    nc = tc.nc
    with ExitStack() as ctx:
        const = ctx.enter_context(tc.tile_pool(name="const", bufs=1))
        ring = ctx.enter_context(tc.tile_pool(name="ring", bufs=8))
        grp = ctx.enter_context(tc.tile_pool(name="grp", bufs=3))
        cod = ctx.enter_context(tc.tile_pool(name="cod", bufs=3))
        st = ctx.enter_context(tc.tile_pool(name="st", bufs=2))
        ep = ctx.enter_context(tc.tile_pool(name="ep", bufs=2))
        tp = ctx.enter_context(tc.psum_pool(name="tp", bufs=4))
        acc = ctx.enter_context(tc.psum_pool(name="acc", bufs=4))
        ctx.enter_context(tc.manual_schedule())

        weights = (W_key, W_value)
        raw_w = {}
        states = {}

        def load_w(v, j, h):
            wr = ring.tile([P, 4096], BF16, tag="ring", name="wr")
            row0 = NT * j + 256 * h
            nc.sync.dma_start(
                out=wr[:].rearrange("p (c k) -> p c k", c=2),
                in_=weights[v][row0 : row0 + 256, :].rearrange("(c p) k -> p c k", p=P),
            )
            raw_w[(v, j, h)] = wr

        def load_states(j):
            tiles = []
            for src in (state_p, state_A, state_B):
                t = st.tile([P, 1024], BF16, tag="st%d" % len(tiles), name="st_t")
                nc.sync.dma_start(
                    out=t[:].rearrange("p (r d) -> p r d", r=2),
                    in_=src.rearrange("(r p) d -> p r d", p=P)[:, :, NT * j : NT * (j + 1)],
                )
                tiles.append(t)
            states[j] = tiles

        mkb = const.tile([P, 32], BF16, name="mkb")
        with nc.allow_non_contiguous_dma(reason="mix coefficients, two neighbouring k to a partition"):
            nc.scalar.dma_start(
                out=mkb[:, 0:16].rearrange("p (a e) -> p a e", e=2),
                in_=time_mix_k.rearrange("o (a p e) -> p (o a) e", a=8, p=P, e=2),
            )
            nc.scalar.dma_start(
                out=mkb[:, 16:32].rearrange("p (a e) -> p a e", e=2),
                in_=time_mix_v.rearrange("o (a p e) -> p (o a) e", a=8, p=P, e=2),
            )
        vec_rows = const.tile([P, D], BF16, name="vec_rows")
        nc.vector.memset(vec_rows[:], 0.0)
        nc.scalar.dma_start(out=vec_rows[0:1, :], in_=time_first.unsqueeze(0))
        nc.scalar.dma_start(out=vec_rows[1:2, :], in_=time_decay.unsqueeze(0))
        x_sb = ring.tile([P, 4096], BF16, tag="ring", name="x_sb")
        sx_sb = ring.tile([P, 4096], BF16, tag="ring", name="sx_sb")
        for g in range(4):
            for dst, src in ((sx_sb, state_x), (x_sb, x)):
                nc.sync.dma_start(
                    out=dst[:, 1024 * g : 1024 * (g + 1)].rearrange("p (r k) -> p r k", r=2),
                    in_=src.rearrange("(r p) k -> p r k", p=P)[:, :, 512 * g : 512 * (g + 1)],
                )
        for v in range(2):
            for h in range(2):
                load_w(v, 0, h)
        load_states(0)
        load_w(0, 1, 0)
        load_w(0, 1, 1)

        ident = const.tile([P, P], F32, name="ident")
        make_identity(nc, ident[:])
        identb = const.tile([P, P], BF16, name="identb")
        make_identity(nc, identb[:])
        nidentb = const.tile([P, P], BF16, name="nidentb")
        nc.vector.tensor_scalar_mul(out=nidentb[:], in0=identb[:], scalar1=-1.0)
        warm_in = const.tile([P, 1], F32, name="warm_in")
        warm_out = const.tile([P, 1], F32, name="warm_out")
        nc.vector.memset(warm_in[:], 0.0)
        nc.scalar.activation(out=warm_out[:], in_=warm_in[:], func=ACT.Exp)
        mkf = const.tile([P, 32], F32, name="mkf")
        nc.vector.tensor_copy(out=mkf[:], in_=mkb[:])

        xg = grp.tile([P, 8192], BF16, tag="grp", name="xg", align_bytes=64)
        sw = sx_sb[:].bitcast(F32)
        for g in range(4):
            sb = tp.tile([P, 512], F32, tag="tp", name="sb")
            for u in range(2):
                for r in range(2):
                    src = 512 * g + 256 * r + 128 * u
                    col = 256 * u + 128 * r
                    nc.tensor.transpose(sb[:, col : col + 128], sw[:, src : src + 128], ident[:])
            sxs = ep.tile([P, 1024], BF16, tag="ndd", name="sxs")
            nc.scalar.copy(out=sxs[:].bitcast(F32), in_=sb[:])
            plns = [ep.tile([P, 1024], BF16, tag="t%d" % (v + 1), name="pln") for v in range(2)]
            for u in range(2):
                dxb = acc.tile([P, 512], F32, tag="acc", name="dxb")
                for e in range(2):
                    for r in range(2):
                        base = 1024 * g + 512 * r + 256 * u
                        col = 256 * e + 128 * r
                        xs = x_sb[:, base : base + 256].rearrange("p (w e) -> p w e", e=2)[:, :, e]
                        ss = sx_sb[:, base : base + 256].rearrange("p (w e) -> p w e", e=2)[:, :, e]
                        nc.tensor.matmul(out=dxb[:, col : col + 128], lhsT=xs, rhs=identb[:], start=True, stop=False)
                        nc.tensor.matmul(out=dxb[:, col : col + 128], lhsT=ss, rhs=nidentb[:], start=False, stop=True)
                for e in range(2):
                    t = 2 * u + e
                    sx_pl = sxs[:, 512 * u : 512 * (u + 1)].rearrange("p (n e) -> p n e", e=2)[:, :, e]
                    for v in range(2):
                        i = 16 * v + 4 * g + t
                        nc.vector.scalar_tensor_tensor(
                            out=plns[v][:, 256 * t : 256 * (t + 1)],
                            in0=dxb[:, 256 * e : 256 * (e + 1)],
                            scalar=mkf[:, i : i + 1],
                            in1=sx_pl,
                            op0=ALU.mult,
                            op1=ALU.add,
                        )
            for v in range(2):
                o0 = 4096 * v + 1024 * g
                nc.gpsimd.tensor_scalar(
                    out=xg[:, o0 : o0 + 1024].rearrange("p (n t) -> p n t", t=4),
                    in0=plns[v][:].rearrange("p (t n) -> p n t", t=4),
                    scalar1=1.0,
                    scalar2=0.0,
                    op0=ALU.mult,
                    op1=ALU.add,
                )
        load_w(1, 1, 0)
        load_w(1, 1, 1)

        xcodes = const.tile([P, 2048], U32, name="xcodes", align_bytes=64)
        xscl = const.tile([P, 2048], U8, name="xscl", align_bytes=64)

        def quantise_x(v):
            nc.vector.quantize_mx(
                out=xcodes[:, 1024 * v : 1024 * (v + 1)].bitcast(FP8X4),
                scales=xscl[:, 1024 * v : 1024 * (v + 1)],
                in_=xg[:, 4096 * v : 4096 * (v + 1)],
            )

        def regroup_w(v, j):
            gt = grp.tile([P, 8192], BF16, tag="grp", name="gt", align_bytes=64)
            gw = gt[:].bitcast(F32).rearrange("p (g d u) -> p g d u", g=4, d=NT, u=2)
            for c in range(4):
                wf = raw_w[(v, j, c // 2)][:].bitcast(F32)
                base = 1024 * (c % 2)
                for hb in range(2):
                    bank = tp.tile([P, 512], F32, tag="tp", name="bank")
                    for gi in range(2):
                        for u in range(2):
                            src = base + 256 * (2 * hb + gi) + 128 * u
                            col = 128 * (2 * gi + u)
                            nc.tensor.transpose(bank[:, col : col + 128], wf[:, src : src + 128], ident[:])
                    nc.scalar.copy(
                        out=gw[:, 2 * hb : 2 * hb + 2, 128 * c : 128 * (c + 1), :],
                        in_=bank[:].rearrange("p (g u d) -> p g d u", g=2, u=2, d=128),
                    )
            return gt

        def quantise_w(gt):
            codes = cod.tile([P, 2048], U32, tag="codes", name="codes", align_bytes=64)
            scl = cod.tile([P, 2048], U8, tag="scl", name="scl", align_bytes=64)
            for hb in range(2):
                nc.vector.quantize_mx(
                    out=codes[:, 1024 * hb : 1024 * (hb + 1)].bitcast(FP8X4),
                    scales=scl[:, 1024 * hb : 1024 * (hb + 1)],
                    in_=gt[:, 4096 * hb : 4096 * (hb + 1)],
                )
            return codes, scl

        def project(v, wq, r):
            codes, scl = wq
            ps = acc.tile([P, NT], F32, tag="acc", name="ps")
            for g in range(4):
                c0 = 1024 * v + 256 * g + 128 * r
                nc.tensor.matmul_mx(
                    out=ps[:],
                    lhsT=xcodes[:, c0 : c0 + 128].bitcast(FP8X4),
                    lhsT_scale=xscl[:, c0 : c0 + 128],
                    rhs=codes[:, NT * g : NT * (g + 1)].bitcast(FP8X4),
                    rhs_scale=scl[:, NT * g : NT * (g + 1)],
                    start=(g == 0),
                    stop=(g == 3),
                )
            return ps

        tfw = const.tile([P, 4096], F32, name="tfw")
        tfw_v = tfw[:].rearrange("p (h d) -> p h d", h=2)

        def spread_vectors(j):
            cols = slice(NT * j, NT * (j + 1))
            spread = []
            for row in range(2):
                ps = tp.tile([P, NT], F32, tag="tp", name="spread_ps")
                nc.tensor.matmul(
                    out=ps[:],
                    lhsT=identb[:, row : row + 1].to_broadcast([P, P]),
                    rhs=vec_rows[:, cols],
                    start=True,
                    stop=True,
                )
                spread.append(ps)
            nc.scalar.copy(out=tfw[:, NT * j : NT * (j + 1)], in_=spread[0][:])
            nc.scalar.activation(out=tfw[:, D + NT * j : D + NT * (j + 1)], in_=spread[1][:], func=ACT.Exp)

        two = "p (h d) -> p h d"

        def store(dst, j, r, src):
            nc.sync.dma_start(out=dst[P * r : P * (r + 1), NT * j : NT * (j + 1)], in_=src)

        def per_row_tile(t, r):
            return t[:, NT * r : NT * (r + 1)]

        def twice(ap):
            return ap.unsqueeze(1).to_broadcast([P, 2, NT])

        def exponents(j, k_ps):
            sp_t = states[j][0]
            nq = [ep.tile([P, NT], F32, tag="nq", name="nq") for r in range(2)]
            ndd = [ep.tile([P, 1024], F32, tag="ndd", name="ndd") for r in range(2)]
            xf1 = [ep.tile([P, 1024], F32, tag="xf0", name="xf1") for r in range(2)]
            xf2 = [ep.tile([P, 1024], F32, tag="xf1", name="xf2") for r in range(2)]
            p2 = [ep.tile([P, NT], F32, tag="p2", name="p2") for r in range(2)]
            for r in range(2):
                nc.vector.tensor_tensor(out=nq[r][:], in0=per_row_tile(sp_t, r), in1=k_ps[r][:], op=ALU.subtract)
            for r in range(2):
                nc.vector.tensor_tensor(
                    out=ndd[r][:].rearrange(two, h=2),
                    in0=twice(nq[r][:]),
                    in1=tfw_v[:, :, NT * j : NT * (j + 1)],
                    op=ALU.subtract,
                )
            for r in range(2):
                nc.scalar.activation(out=xf1[r][:], in_=ndd[r][:], func=ACT.Exp)
            for r in range(2):
                nc.scalar.activation(out=xf2[r][:], in_=ndd[r][:], func=ACT.Exp, scale=-1.0)
            for r in range(2):
                nc.vector.scalar_tensor_tensor(
                    out=p2[r][:], in0=ndd[r][:, NT : 2 * NT], scalar=0.0, in1=k_ps[r][:], op0=ALU.max, op1=ALU.add
                )
                store(out_4, j, r, p2[r][:])
            return xf1, xf2

        def numerators(j, v_ps, xf1, xf2):
            a_t = states[j][1]
            t1 = [ep.tile([P, 1024], F32, tag="t1", name="t1") for r in range(2)]
            t2 = [ep.tile([P, 1024], F32, tag="t2", name="t2") for r in range(2)]
            for r in range(2):
                nc.vector.scalar_tensor_tensor(
                    out=t1[r][:].rearrange(two, h=2),
                    in0=xf1[r][:].rearrange(two, h=2),
                    scalar=1.0,
                    in1=twice(per_row_tile(a_t, r)),
                    op0=ALU.min,
                    op1=ALU.mult,
                )
            for r in range(2):
                nc.vector.scalar_tensor_tensor(
                    out=t2[r][:].rearrange(two, h=2),
                    in0=xf2[r][:].rearrange(two, h=2),
                    scalar=1.0,
                    in1=twice(v_ps[r][:]),
                    op0=ALU.min,
                    op1=ALU.mult,
                )
            for r in range(2):
                nc.vector.tensor_tensor(out=t1[r][:], in0=t1[r][:], in1=t2[r][:], op=ALU.add)
                store(out_0, j, r, t1[r][:, 0:NT])
                store(out_2, j, r, t1[r][:, NT : 2 * NT])

        def denominators(j, xf1, xf2):
            b_t = states[j][2]
            for r in range(2):
                nc.vector.scalar_tensor_tensor(
                    out=xf1[r][:].rearrange(two, h=2),
                    in0=xf1[r][:].rearrange(two, h=2),
                    scalar=1.0,
                    in1=twice(per_row_tile(b_t, r)),
                    op0=ALU.min,
                    op1=ALU.mult,
                )
            for r in range(2):
                nc.vector.scalar_tensor_tensor(
                    out=xf2[r][:], in0=xf2[r][:], scalar=1.0, in1=xf1[r][:], op0=ALU.min, op1=ALU.add
                )
                store(out_1, j, r, xf2[r][:, 0:NT])
                store(out_3, j, r, xf2[r][:, NT : 2 * NT])

        gt_k = regroup_w(0, 0)
        load_states(1)
        spread_vectors(0)
        wq_k = quantise_w(gt_k)
        quantise_x(0)
        gt_v = regroup_w(1, 0)
        wq_v = quantise_w(gt_v)
        quantise_x(1)
        k_ps = [project(0, wq_k, r) for r in range(2)]
        v_ps = [project(1, wq_v, r) for r in range(2)]

        for j in range(TILES):
            xf1, xf2 = exponents(j, k_ps)
            if j + 1 < TILES:
                spread_vectors(j + 1)
            if j + 2 < TILES:
                load_w(0, j + 2, 0)
                load_w(0, j + 2, 1)
            if j + 1 < TILES:
                gt_k = regroup_w(0, j + 1)
                gt_v = regroup_w(1, j + 1)
            numerators(j, v_ps, xf1, xf2)
            if j + 2 < TILES:
                load_w(1, j + 2, 0)
                load_w(1, j + 2, 1)
            denominators(j, xf1, xf2)
            if j + 2 < TILES:
                load_states(j + 2)
            if j + 1 < TILES:
                wq_k = quantise_w(gt_k)
                wq_v = quantise_w(gt_v)
                k_ps = [project(0, wq_k, r) for r in range(2)]
                v_ps = [project(1, wq_v, r) for r in range(2)]
